import numpy as np
import ml_dtypes

BF16 = ml_dtypes.bfloat16


def bf(x):
    return np.asarray(x, np.float32).astype(BF16)


def f32(x):
    return np.asarray(x, np.float32)


def f64(x):
    return np.asarray(x).astype(np.float64)


def striped(idx):
    return np.tile(idx.reshape(-1, 16).T, (8, 1))


C, S, N = 1024, 256, 128
EPS = 1e-5


def setup_inputs():
    emb = (0.5 + np.random.random((1, S))) * np.random.standard_normal((C, S)) + 0.5 * np.random.standard_normal((1, S))
    gain = 1.0 + 0.1 * np.random.standard_normal((C, 1))
    bias = 0.1 * np.random.standard_normal((C, 1))
    wlm = np.random.standard_normal((C, S)) / np.sqrt(C)
    idx = np.random.permutation(np.tile(np.arange(S), 2))[:N]
    return {"emb": f32(emb), "gain": f32(gain), "bias": f32(bias), "wlm": bf(wlm), "offs": striped(idx)}


def reference(emb, gain, bias, wlm, offs):
    idx = offs[:16].T.reshape(-1)
    e = f64(emb)[:, idx]
    mu = e.mean(axis=0, keepdims=True)
    var = ((e - mu) ** 2).mean(axis=0, keepdims=True)
    y = (e - mu) / np.sqrt(var + EPS) * f64(gain) + f64(bias)
    return f64(wlm).T @ y

@@ -1,0 +1,89 @@
+import concourse.mybir as mybir
+
+F32 = mybir.dt.float32
+BF16 = mybir.dt.bfloat16
+U16 = mybir.dt.uint16
+ACT = mybir.ActivationFunctionType
+ALU = mybir.AluOpType
+
+P = 128
+C = 1024
+S = 256
+V = 256
+N = 128
+NB = C // P
+NH = V // P
+EPS = 1e-5
+
+FLOPS = 2 * C * V * N
+
+
+def tile_gatedattentiontransformer_kernel(tc, emb, gain, bias, wlm, offs, out):
+    nc = tc.nc
+    with (
+        tc.tile_pool(name="held", bufs=1) as held,
+        tc.tile_pool(name="blocks", bufs=NB) as blocks,
+        tc.psum_pool(name="psum", bufs=1) as psum,
+    ):
+        offsets = held.tile([P, N // 16], U16, name="offsets")
+        nc.sync.dma_start(offsets[:], offs)
+
+        emb_blocks = emb.rearrange("(p b) s -> b p s", b=NB)
+        tables = []
+        for b in range(NB):
+            table = blocks.tile([P, S], F32, name="table")
+            queue = nc.sync if b % 2 == 0 else nc.scalar
+            queue.dma_start(table[:], emb_blocks[b])
+            tables.append(table)
+        gain_sb = held.tile([P, NB], F32, name="gain_sb")
+        nc.gpsimd.dma_start(gain_sb[:], gain.rearrange("(p b) one -> p (b one)", b=NB))
+        bias_sb = held.tile([P, NB], F32, name="bias_sb")
+        nc.gpsimd.dma_start(bias_sb[:], bias.rearrange("(p b) one -> p (b one)", b=NB))
+        wlm_sb = held.tile([P, NB, V], BF16, name="wlm_sb")
+        nc.sync.dma_start(wlm_sb[:], wlm.rearrange("(p b) v -> p b v", b=NB))
+
+        averager = held.tile([P, P], F32, name="averager")
+        nc.vector.memset(averager[:], 1.0 / C)
+        eps = held.tile([P, 1], F32, name="eps")
+        nc.vector.memset(eps[:], EPS)
+
+        mean = psum.tile([P, N], F32, name="mean")
+        picked = []
+        for b in range(NB):
+            e = blocks.tile([P, N], F32, name="e")
+            nc.scalar.activation(e[:], tables[b][:].indirect(offsets[:]), ACT.Copy)
+            nc.tensor.matmul(mean[:], averager[:], e[:], start=(b == 0), stop=(b == NB - 1))
+            picked.append(e)
+
+        var = psum.tile([P, N], F32, name="var")
+        centred = []
+        for b in range(NB):
+            d = blocks.tile([P, N], F32, name="d")
+            nc.vector.tensor_tensor(d[:], picked[b][:], mean[:], ALU.subtract)
+            sq = blocks.tile([P, N], F32, name="sq")
+            nc.scalar.activation(sq[:], d[:], ACT.Square)
+            nc.tensor.matmul(var[:], averager[:], sq[:], start=(b == 0), stop=(b == NB - 1))
+            centred.append(d)
+
+        rstd = held.tile([P, N], F32, name="rstd")
+        nc.scalar.activation(rstd[:], var[:], ACT.Abs_reciprocal_sqrt, bias=eps[:])
+
+        logits = [psum.tile([P, N], F32, name=f"logits{h}") for h in range(NH)]
+        for b in range(NB):
+            z = blocks.tile([P, N], F32, name="z")
+            nc.vector.tensor_tensor(z[:], centred[b][:], rstd[:], ALU.mult)
+            y = blocks.tile([P, N], BF16, name="y")
+            nc.scalar.activation(
+                y[:], z[:], ACT.Identity, bias=bias_sb[:, b : b + 1], scale=gain_sb[:, b : b + 1]
+            )
+            for h in range(NH):
+                nc.tensor.matmul(
+                    logits[h][:], wlm_sb[:, b, h * P : (h + 1) * P], y[:], start=(b == 0), stop=(b == NB - 1)
+                )
+
+        staged0 = held.tile([P, N], F32, name="staged0")
+        nc.vector.tensor_copy(staged0[:], logits[0][:])
+        nc.sync.dma_start(out[0:P, :], staged0[:])
+        staged1 = held.tile([P, N], F32, name="staged1")
+        nc.scalar.copy(staged1[:], logits[1][:])
+        nc.scalar.dma_start(out[P : 2 * P, :], staged1[:])

@@ -47,6 +47,9 @@ def tile_gatedattentiontransformer_kernel(tc, emb, gain, bias, wlm, offs, out):
         eps = held.tile([P, 1], F32, name="eps")
         nc.vector.memset(eps[:], EPS)
 
+        warm = held.tile([P, 1], F32, name="warm")
+        nc.scalar.activation(warm[:], eps[:], ACT.Abs_reciprocal_sqrt)
+
         mean = psum.tile([P, N], F32, name="mean")
         picked = []
         for b in range(NB):

@@ -50,23 +50,33 @@ def tile_gatedattentiontransformer_kernel(tc, emb, gain, bias, wlm, offs, out):
         warm = held.tile([P, 1], F32, name="warm")
         nc.scalar.activation(warm[:], eps[:], ACT.Abs_reciprocal_sqrt)
 
+        def add_pair_to(average, blocks_of_a_sum, k):
+            pair = blocks.tile([P, N], F32, name="pair")
+            nc.vector.tensor_tensor(pair[:], blocks_of_a_sum[2 * k][:], blocks_of_a_sum[2 * k + 1][:], ALU.add)
+            nc.tensor.matmul(average[:], averager[:], pair[:], start=(k == 0), stop=(k == NB // 2 - 1))
+
         mean = psum.tile([P, N], F32, name="mean")
         picked = []
         for b in range(NB):
             e = blocks.tile([P, N], F32, name="e")
             nc.scalar.activation(e[:], tables[b][:].indirect(offsets[:]), ACT.Copy)
-            nc.tensor.matmul(mean[:], averager[:], e[:], start=(b == 0), stop=(b == NB - 1))
             picked.append(e)
+            if b % 2 == 1:
+                add_pair_to(mean, picked, b // 2)
 
         var = psum.tile([P, N], F32, name="var")
         centred = []
+        squares = []
         for b in range(NB):
             d = blocks.tile([P, N], F32, name="d")
             nc.vector.tensor_tensor(d[:], picked[b][:], mean[:], ALU.subtract)
+            centred.append(d)
             sq = blocks.tile([P, N], F32, name="sq")
             nc.scalar.activation(sq[:], d[:], ACT.Square)
-            nc.tensor.matmul(var[:], averager[:], sq[:], start=(b == 0), stop=(b == NB - 1))
-            centred.append(d)
+            squares.append(sq)
+            if b % 2 == 1 and b >= 3:
+                add_pair_to(var, squares, b // 2 - 1)
+        add_pair_to(var, squares, NB // 2 - 1)
 
         rstd = held.tile([P, N], F32, name="rstd")
         nc.scalar.activation(rstd[:], var[:], ACT.Abs_reciprocal_sqrt, bias=eps[:])

@@ -36,9 +36,9 @@ def tile_gatedattentiontransformer_kernel(tc, emb, gain, bias, wlm, offs, out):
             queue.dma_start(table[:], emb_blocks[b])
             tables.append(table)
         gain_sb = held.tile([P, NB], F32, name="gain_sb")
-        nc.gpsimd.dma_start(gain_sb[:], gain.rearrange("(p b) one -> p (b one)", b=NB))
+        nc.scalar.dma_start(gain_sb[:], gain.rearrange("(p b) one -> p (b one)", b=NB))
         bias_sb = held.tile([P, NB], F32, name="bias_sb")
-        nc.gpsimd.dma_start(bias_sb[:], bias.rearrange("(p b) one -> p (b one)", b=NB))
+        nc.scalar.dma_start(bias_sb[:], bias.rearrange("(p b) one -> p (b one)", b=NB))
         wlm_sb = held.tile([P, NB, V], BF16, name="wlm_sb")
         nc.sync.dma_start(wlm_sb[:], wlm.rearrange("(p b) v -> p b v", b=NB))
 
@@ -50,33 +50,23 @@ def tile_gatedattentiontransformer_kernel(tc, emb, gain, bias, wlm, offs, out):
         warm = held.tile([P, 1], F32, name="warm")
         nc.scalar.activation(warm[:], eps[:], ACT.Abs_reciprocal_sqrt)
 
-        def add_pair_to(average, blocks_of_a_sum, k):
-            pair = blocks.tile([P, N], F32, name="pair")
-            nc.vector.tensor_tensor(pair[:], blocks_of_a_sum[2 * k][:], blocks_of_a_sum[2 * k + 1][:], ALU.add)
-            nc.tensor.matmul(average[:], averager[:], pair[:], start=(k == 0), stop=(k == NB // 2 - 1))
-
         mean = psum.tile([P, N], F32, name="mean")
         picked = []
         for b in range(NB):
             e = blocks.tile([P, N], F32, name="e")
             nc.scalar.activation(e[:], tables[b][:].indirect(offsets[:]), ACT.Copy)
+            nc.tensor.matmul(mean[:], averager[:], e[:], start=(b == 0), stop=(b == NB - 1))
             picked.append(e)
-            if b % 2 == 1:
-                add_pair_to(mean, picked, b // 2)
 
         var = psum.tile([P, N], F32, name="var")
         centred = []
-        squares = []
         for b in range(NB):
             d = blocks.tile([P, N], F32, name="d")
             nc.vector.tensor_tensor(d[:], picked[b][:], mean[:], ALU.subtract)
-            centred.append(d)
             sq = blocks.tile([P, N], F32, name="sq")
             nc.scalar.activation(sq[:], d[:], ACT.Square)
-            squares.append(sq)
-            if b % 2 == 1 and b >= 3:
-                add_pair_to(var, squares, b // 2 - 1)
-        add_pair_to(var, squares, NB // 2 - 1)
+            nc.tensor.matmul(var[:], averager[:], sq[:], start=(b == 0), stop=(b == NB - 1))
+            centred.append(d)
 
         rstd = held.tile([P, N], F32, name="rstd")
         nc.scalar.activation(rstd[:], var[:], ACT.Abs_reciprocal_sqrt, bias=eps[:])

@@ -14,6 +14,7 @@ N = 128
 NB = C // P
 NH = V // P
 EPS = 1e-5
+WARMING_MATMULS = 6
 
 FLOPS = 2 * C * V * N
 
@@ -49,6 +50,10 @@ def tile_gatedattentiontransformer_kernel(tc, emb, gain, bias, wlm, offs, out):
 
         warm = held.tile([P, 1], F32, name="warm")
         nc.scalar.activation(warm[:], eps[:], ACT.Abs_reciprocal_sqrt)
+
+        idle_product = psum.tile([P, P], F32, name="idle_product")
+        for i in range(WARMING_MATMULS):
+            nc.tensor.matmul(idle_product[:], averager[:], averager[:], start=True, stop=True)
 
         mean = psum.tile([P, N], F32, name="mean")
         picked = []

@@ -45,6 +45,8 @@ def tile_gatedattentiontransformer_kernel(tc, emb, gain, bias, wlm, offs, out):
 
         averager = held.tile([P, P], F32, name="averager")
         nc.vector.memset(averager[:], 1.0 / C)
+        averager_bf = held.tile([P, P], BF16, name="averager_bf")
+        nc.vector.memset(averager_bf[:], 1.0 / C)
         eps = held.tile([P, 1], F32, name="eps")
         nc.vector.memset(eps[:], EPS)
 
@@ -68,9 +70,9 @@ def tile_gatedattentiontransformer_kernel(tc, emb, gain, bias, wlm, offs, out):
         for b in range(NB):
             d = blocks.tile([P, N], F32, name="d")
             nc.vector.tensor_tensor(d[:], picked[b][:], mean[:], ALU.subtract)
-            sq = blocks.tile([P, N], F32, name="sq")
+            sq = blocks.tile([P, N], BF16, name="sq")
             nc.scalar.activation(sq[:], d[:], ACT.Square)
-            nc.tensor.matmul(var[:], averager[:], sq[:], start=(b == 0), stop=(b == NB - 1))
+            nc.tensor.matmul(var[:], averager_bf[:], sq[:], start=(b == 0), stop=(b == NB - 1))
             centred.append(d)
 
         rstd = held.tile([P, N], F32, name="rstd")

@@ -15,6 +15,7 @@ NB = C // P
 NH = V // P
 EPS = 1e-5
 WARMING_MATMULS = 6
+BRIDGING_MATMULS = 2
 
 FLOPS = 2 * C * V * N
 
@@ -54,8 +55,12 @@ def tile_gatedattentiontransformer_kernel(tc, emb, gain, bias, wlm, offs, out):
         nc.scalar.activation(warm[:], eps[:], ACT.Abs_reciprocal_sqrt)
 
         idle_product = psum.tile([P, P], F32, name="idle_product")
-        for i in range(WARMING_MATMULS):
-            nc.tensor.matmul(idle_product[:], averager[:], averager[:], start=True, stop=True)
+
+        def keep_tensor_engine_busy(matmuls):
+            for i in range(matmuls):
+                nc.tensor.matmul(idle_product[:], averager[:], averager[:], start=True, stop=True)
+
+        keep_tensor_engine_busy(WARMING_MATMULS)
 
         mean = psum.tile([P, N], F32, name="mean")
         picked = []
@@ -64,6 +69,8 @@ def tile_gatedattentiontransformer_kernel(tc, emb, gain, bias, wlm, offs, out):
             nc.scalar.activation(e[:], tables[b][:].indirect(offsets[:]), ACT.Copy)
             nc.tensor.matmul(mean[:], averager[:], e[:], start=(b == 0), stop=(b == NB - 1))
             picked.append(e)
+
+        keep_tensor_engine_busy(BRIDGING_MATMULS)
 
         var = psum.tile([P, N], F32, name="var")
         centred = []
@@ -74,6 +81,8 @@ def tile_gatedattentiontransformer_kernel(tc, emb, gain, bias, wlm, offs, out):
             nc.scalar.activation(sq[:], d[:], ACT.Square)
             nc.tensor.matmul(var[:], averager_bf[:], sq[:], start=(b == 0), stop=(b == NB - 1))
             centred.append(d)
+
+        keep_tensor_engine_busy(BRIDGING_MATMULS)
 
         rstd = held.tile([P, N], F32, name="rstd")
         nc.scalar.activation(rstd[:], var[:], ACT.Abs_reciprocal_sqrt, bias=eps[:])

@@ -14,6 +14,7 @@ N = 128
 NB = C // P
 NH = V // P
 EPS = 1e-5
+
 WARMING_MATMULS = 6
 BRIDGING_MATMULS = 2
 
@@ -51,16 +52,16 @@ def tile_gatedattentiontransformer_kernel(tc, emb, gain, bias, wlm, offs, out):
         eps = held.tile([P, 1], F32, name="eps")
         nc.vector.memset(eps[:], EPS)
 
-        warm = held.tile([P, 1], F32, name="warm")
-        nc.scalar.activation(warm[:], eps[:], ACT.Abs_reciprocal_sqrt)
+        scratch = held.tile([P, 1], F32, name="scratch")
+        nc.scalar.activation(scratch[:], eps[:], ACT.Abs_reciprocal_sqrt)
 
         idle_product = psum.tile([P, P], F32, name="idle_product")
 
-        def keep_tensor_engine_busy(matmuls):
+        def keep_tensor_engine_busy(matmuls, moving):
             for i in range(matmuls):
-                nc.tensor.matmul(idle_product[:], averager[:], averager[:], start=True, stop=True)
+                nc.tensor.matmul(idle_product[:], averager[:], moving[:], start=True, stop=True)
 
-        keep_tensor_engine_busy(WARMING_MATMULS)
+        keep_tensor_engine_busy(WARMING_MATMULS, averager)
 
         mean = psum.tile([P, N], F32, name="mean")
         picked = []
@@ -69,8 +70,7 @@ def tile_gatedattentiontransformer_kernel(tc, emb, gain, bias, wlm, offs, out):
             nc.scalar.activation(e[:], tables[b][:].indirect(offsets[:]), ACT.Copy)
             nc.tensor.matmul(mean[:], averager[:], e[:], start=(b == 0), stop=(b == NB - 1))
             picked.append(e)
-
-        keep_tensor_engine_busy(BRIDGING_MATMULS)
+        keep_tensor_engine_busy(BRIDGING_MATMULS, picked[NB - 1])
 
         var = psum.tile([P, N], F32, name="var")
         centred = []
@@ -82,10 +82,9 @@ def tile_gatedattentiontransformer_kernel(tc, emb, gain, bias, wlm, offs, out):
             nc.tensor.matmul(var[:], averager_bf[:], sq[:], start=(b == 0), stop=(b == NB - 1))
             centred.append(d)
 
-        keep_tensor_engine_busy(BRIDGING_MATMULS)
-
         rstd = held.tile([P, N], F32, name="rstd")
         nc.scalar.activation(rstd[:], var[:], ACT.Abs_reciprocal_sqrt, bias=eps[:])
+        keep_tensor_engine_busy(BRIDGING_MATMULS, rstd)
 
         logits = [psum.tile([P, N], F32, name=f"logits{h}") for h in range(NH)]
         for b in range(NB):

@@ -35,13 +35,12 @@ def tile_gatedattentiontransformer_kernel(tc, emb, gain, bias, wlm, offs, out):
         tables = []
         for b in range(NB):
             table = blocks.tile([P, S], F32, name="table")
-            queue = nc.sync if b % 2 == 0 else nc.scalar
-            queue.dma_start(table[:], emb_blocks[b])
+            nc.sync.dma_start(table[:], emb_blocks[b])
             tables.append(table)
         gain_sb = held.tile([P, NB], F32, name="gain_sb")
-        nc.scalar.dma_start(gain_sb[:], gain.rearrange("(p b) one -> p (b one)", b=NB))
+        nc.sync.dma_start(gain_sb[:], gain.rearrange("(p b) one -> p (b one)", b=NB))
         bias_sb = held.tile([P, NB], F32, name="bias_sb")
-        nc.scalar.dma_start(bias_sb[:], bias.rearrange("(p b) one -> p (b one)", b=NB))
+        nc.sync.dma_start(bias_sb[:], bias.rearrange("(p b) one -> p (b one)", b=NB))
         wlm_sb = held.tile([P, NB, V], BF16, name="wlm_sb")
         nc.sync.dma_start(wlm_sb[:], wlm.rearrange("(p b) v -> p b v", b=NB))
 

@@ -15,7 +15,7 @@ NB = C // P
 NH = V // P
 EPS = 1e-5
 
-WARMING_MATMULS = 6
+WARMING_MATMULS = 3
 BRIDGING_MATMULS = 2
 
 FLOPS = 2 * C * V * N

@@ -94,13 +94,9 @@ def tile_gatedattentiontransformer_kernel(tc, emb, gain, bias, wlm, offs, out):
                 y[:], z[:], ACT.Identity, bias=bias_sb[:, b : b + 1], scale=gain_sb[:, b : b + 1]
             )
             for h in range(NH):
-                nc.tensor.matmul(
-                    logits[h][:], wlm_sb[:, b, h * P : (h + 1) * P], y[:], start=(b == 0), stop=(b == NB - 1)
-                )
+                nc.tensor.matmul(logits[h][:], wlm_sb[:, b, h:V:NH], y[:], start=(b == 0), stop=(b == NB - 1))
 
-        staged0 = held.tile([P, N], F32, name="staged0")
-        nc.vector.tensor_copy(staged0[:], logits[0][:])
-        nc.sync.dma_start(out[0:P, :], staged0[:])
-        staged1 = held.tile([P, N], F32, name="staged1")
-        nc.scalar.copy(staged1[:], logits[1][:])
-        nc.scalar.dma_start(out[P : 2 * P, :], staged1[:])
+        staged = held.tile([P, NH, N], F32, name="staged")
+        nc.vector.tensor_copy(staged[:, 0, :], logits[0][:])
+        nc.scalar.copy(staged[:, 1, :], logits[1][:])
+        nc.sync.dma_start(out.rearrange("(m h) j -> m h j", h=NH), staged[:])

@@ -16,7 +16,6 @@ NH = V // P
 EPS = 1e-5
 
 WARMING_MATMULS = 3
-BRIDGING_MATMULS = 2
 
 FLOPS = 2 * C * V * N
 
@@ -55,12 +54,8 @@ def tile_gatedattentiontransformer_kernel(tc, emb, gain, bias, wlm, offs, out):
         nc.scalar.activation(scratch[:], eps[:], ACT.Abs_reciprocal_sqrt)
 
         idle_product = psum.tile([P, P], F32, name="idle_product")
-
-        def keep_tensor_engine_busy(matmuls, moving):
-            for i in range(matmuls):
-                nc.tensor.matmul(idle_product[:], averager[:], moving[:], start=True, stop=True)
-
-        keep_tensor_engine_busy(WARMING_MATMULS, averager)
+        for i in range(WARMING_MATMULS):
+            nc.tensor.matmul(idle_product[:], averager[:], averager[:], start=True, stop=True)
 
         mean = psum.tile([P, N], F32, name="mean")
         picked = []
@@ -69,7 +64,6 @@ def tile_gatedattentiontransformer_kernel(tc, emb, gain, bias, wlm, offs, out):
             nc.scalar.activation(e[:], tables[b][:].indirect(offsets[:]), ACT.Copy)
             nc.tensor.matmul(mean[:], averager[:], e[:], start=(b == 0), stop=(b == NB - 1))
             picked.append(e)
-        keep_tensor_engine_busy(BRIDGING_MATMULS, picked[NB - 1])
 
         var = psum.tile([P, N], F32, name="var")
         centred = []
@@ -83,7 +77,6 @@ def tile_gatedattentiontransformer_kernel(tc, emb, gain, bias, wlm, offs, out):
 
         rstd = held.tile([P, N], F32, name="rstd")
         nc.scalar.activation(rstd[:], var[:], ACT.Abs_reciprocal_sqrt, bias=eps[:])
-        keep_tensor_engine_busy(BRIDGING_MATMULS, rstd)
 
         logits = [psum.tile([P, N], F32, name=f"logits{h}") for h in range(NH)]
         for b in range(NB):

@@ -13,6 +13,9 @@ V = 256
 N = 128
 NB = C // P
 NH = V // P
+HALVES = 2
+T = N // HALVES
+PAIR = 2
 EPS = 1e-5
 
 WARMING_MATMULS = 3
@@ -58,36 +61,60 @@ def tile_gatedattentiontransformer_kernel(tc, emb, gain, bias, wlm, offs, out):
             nc.tensor.matmul(idle_product[:], averager[:], averager[:], start=True, stop=True)
 
         mean = psum.tile([P, N], F32, name="mean")
-        picked = []
+        e = held.tile([P, NB, N], F32, name="e")
         for b in range(NB):
-            e = blocks.tile([P, N], F32, name="e")
-            nc.scalar.activation(e[:], tables[b][:].indirect(offsets[:]), ACT.Copy)
-            nc.tensor.matmul(mean[:], averager[:], e[:], start=(b == 0), stop=(b == NB - 1))
-            picked.append(e)
+            nc.scalar.activation(e[:, b, :], tables[b][:].indirect(offsets[:]), ACT.Copy)
+            nc.tensor.matmul(mean[:], averager[:], e[:, b, :], start=(b == 0), stop=(b == NB - 1))
 
-        var = psum.tile([P, N], F32, name="var")
-        centred = []
-        for b in range(NB):
-            d = blocks.tile([P, N], F32, name="d")
-            nc.vector.tensor_tensor(d[:], picked[b][:], mean[:], ALU.subtract)
-            sq = blocks.tile([P, N], BF16, name="sq")
-            nc.scalar.activation(sq[:], d[:], ACT.Square)
-            nc.tensor.matmul(var[:], averager_bf[:], sq[:], start=(b == 0), stop=(b == NB - 1))
-            centred.append(d)
-
-        rstd = held.tile([P, N], F32, name="rstd")
-        nc.scalar.activation(rstd[:], var[:], ACT.Abs_reciprocal_sqrt, bias=eps[:])
-
+        d = held.tile([P, NB, N], F32, name="d")
+        sq = held.tile([P, NB, N], BF16, name="sq")
+        z = held.tile([P, NB, N], F32, name="z")
+        y = held.tile([P, NB, N], BF16, name="y")
+        var = [psum.tile([P, T], F32, name=f"var{t}") for t in range(HALVES)]
+        rstd = [held.tile([P, T], F32, name=f"rstd{t}") for t in range(HALVES)]
         logits = [psum.tile([P, N], F32, name=f"logits{h}") for h in range(NH)]
-        for b in range(NB):
-            z = blocks.tile([P, N], F32, name="z")
-            nc.vector.tensor_tensor(z[:], centred[b][:], rstd[:], ALU.mult)
-            y = blocks.tile([P, N], BF16, name="y")
-            nc.scalar.activation(
-                y[:], z[:], ACT.Identity, bias=bias_sb[:, b : b + 1], scale=gain_sb[:, b : b + 1]
+
+        def centre_and_square(t, first):
+            pair = slice(first, first + PAIR)
+            half = slice(t * T, (t + 1) * T)
+            nc.vector.tensor_tensor(
+                d[:, pair, half], e[:, pair, half], mean[:, half].unsqueeze(1).to_broadcast([P, PAIR, T]), ALU.subtract
             )
-            for h in range(NH):
-                nc.tensor.matmul(logits[h][:], wlm_sb[:, b, h:V:NH], y[:], start=(b == 0), stop=(b == NB - 1))
+            nc.scalar.activation(sq[:, pair, half], d[:, pair, half], ACT.Square)
+            for b in range(first, first + PAIR):
+                nc.tensor.matmul(var[t][:], averager_bf[:], sq[:, b, half], start=(b == 0), stop=(b == NB - 1))
+
+        def take_rstd(t):
+            nc.scalar.activation(rstd[t][:], var[t][:], ACT.Abs_reciprocal_sqrt, bias=eps[:])
+
+        def normalise_and_project(t, first):
+            pair = slice(first, first + PAIR)
+            half = slice(t * T, (t + 1) * T)
+            nc.vector.tensor_tensor(
+                z[:, pair, half], d[:, pair, half], rstd[t][:].unsqueeze(1).to_broadcast([P, PAIR, T]), ALU.mult
+            )
+            for b in range(first, first + PAIR):
+                nc.scalar.activation(
+                    y[:, b, half], z[:, b, half], ACT.Identity, bias=bias_sb[:, b : b + 1], scale=gain_sb[:, b : b + 1]
+                )
+                for h in range(NH):
+                    nc.tensor.matmul(
+                        logits[h][:, half], wlm_sb[:, b, h:V:NH], y[:, b, half], start=(b == 0), stop=(b == NB - 1)
+                    )
+
+        firsts = range(0, NB, PAIR)
+        for first in firsts:
+            centre_and_square(0, first)
+        for first in firsts:
+            centre_and_square(1, first)
+            if first == 0:
+                take_rstd(0)
+        for first in firsts:
+            normalise_and_project(0, first)
+            if first == 0:
+                take_rstd(1)
+        for first in firsts:
+            normalise_and_project(1, first)
 
         staged = held.tile([P, NH, N], F32, name="staged")
         nc.vector.tensor_copy(staged[:, 0, :], logits[0][:])

@@ -94,15 +94,22 @@ def tile_gatedattentiontransformer_kernel(tc, emb, gain, bias, wlm, offs, out):
                 z[:, pair, half], d[:, pair, half], rstd[t][:].unsqueeze(1).to_broadcast([P, PAIR, T]), ALU.mult
             )
             for b in range(first, first + PAIR):
+                if t == HALVES - 1 and b >= NB // 2:
+                    left_to_vector.append(b)
+                    continue
                 nc.scalar.activation(
                     y[:, b, half], z[:, b, half], ACT.Identity, bias=bias_sb[:, b : b + 1], scale=gain_sb[:, b : b + 1]
                 )
-                for h in range(NH):
-                    nc.tensor.matmul(
-                        logits[h][:, half], wlm_sb[:, b, h:V:NH], y[:, b, half], start=(b == 0), stop=(b == NB - 1)
-                    )
+                project(b, half)
+
+        def project(b, half):
+            for h in range(NH):
+                nc.tensor.matmul(
+                    logits[h][:, half], wlm_sb[:, b, h:V:NH], y[:, b, half], start=(b == 0), stop=(b == NB - 1)
+                )
 
         firsts = range(0, NB, PAIR)
+        left_to_vector = []
         for first in firsts:
             centre_and_square(0, first)
         for first in firsts:
@@ -115,6 +122,12 @@ def tile_gatedattentiontransformer_kernel(tc, emb, gain, bias, wlm, offs, out):
                 take_rstd(1)
         for first in firsts:
             normalise_and_project(1, first)
+        last_half = slice(N - T, N)
+        for b in left_to_vector:
+            nc.vector.tensor_scalar(
+                y[:, b, last_half], z[:, b, last_half], gain_sb[:, b : b + 1], bias_sb[:, b : b + 1], ALU.mult, ALU.add
+            )
+            project(b, last_half)
 
         staged = held.tile([P, NH, N], F32, name="staged")
         nc.vector.tensor_copy(staged[:, 0, :], logits[0][:])

@@ -13,9 +13,11 @@ V = 256
 N = 128
 NB = C // P
 NH = V // P
+QUARTERS = 4
+Q = N // QUARTERS
+GROUP = 4
 HALVES = 2
 T = N // HALVES
-PAIR = 2
 EPS = 1e-5
 
 WARMING_MATMULS = 3
@@ -70,64 +72,62 @@ def tile_gatedattentiontransformer_kernel(tc, emb, gain, bias, wlm, offs, out):
         sq = held.tile([P, NB, N], BF16, name="sq")
         z = held.tile([P, NB, N], F32, name="z")
         y = held.tile([P, NB, N], BF16, name="y")
-        var = [psum.tile([P, T], F32, name=f"var{t}") for t in range(HALVES)]
-        rstd = [held.tile([P, T], F32, name=f"rstd{t}") for t in range(HALVES)]
+        var = [psum.tile([P, Q], F32, name=f"var{q}") for q in range(QUARTERS)]
+        rstd = [held.tile([P, Q], F32, name=f"rstd{q}") for q in range(QUARTERS)]
         logits = [psum.tile([P, N], F32, name=f"logits{h}") for h in range(NH)]
 
-        def centre_and_square(t, first):
-            pair = slice(first, first + PAIR)
-            half = slice(t * T, (t + 1) * T)
+        def centre_and_square(q, first):
+            group = slice(first, first + GROUP)
+            quarter = slice(q * Q, (q + 1) * Q)
             nc.vector.tensor_tensor(
-                d[:, pair, half], e[:, pair, half], mean[:, half].unsqueeze(1).to_broadcast([P, PAIR, T]), ALU.subtract
+                d[:, group, quarter],
+                e[:, group, quarter],
+                mean[:, quarter].unsqueeze(1).to_broadcast([P, GROUP, Q]),
+                ALU.subtract,
             )
-            nc.scalar.activation(sq[:, pair, half], d[:, pair, half], ACT.Square)
-            for b in range(first, first + PAIR):
-                nc.tensor.matmul(var[t][:], averager_bf[:], sq[:, b, half], start=(b == 0), stop=(b == NB - 1))
+            nc.scalar.activation(sq[:, group, quarter], d[:, group, quarter], ACT.Square)
+            for b in range(first, first + GROUP):
+                nc.tensor.matmul(var[q][:], averager_bf[:], sq[:, b, quarter], start=(b == 0), stop=(b == NB - 1))
 
-        def take_rstd(t):
-            nc.scalar.activation(rstd[t][:], var[t][:], ACT.Abs_reciprocal_sqrt, bias=eps[:])
+        def take_rstd(q):
+            nc.scalar.activation(rstd[q][:], var[q][:], ACT.Abs_reciprocal_sqrt, bias=eps[:])
 
-        def normalise_and_project(t, first):
-            pair = slice(first, first + PAIR)
-            half = slice(t * T, (t + 1) * T)
+        def normalise(q, first):
+            group = slice(first, first + GROUP)
+            quarter = slice(q * Q, (q + 1) * Q)
             nc.vector.tensor_tensor(
-                z[:, pair, half], d[:, pair, half], rstd[t][:].unsqueeze(1).to_broadcast([P, PAIR, T]), ALU.mult
+                z[:, group, quarter],
+                d[:, group, quarter],
+                rstd[q][:].unsqueeze(1).to_broadcast([P, GROUP, Q]),
+                ALU.mult,
             )
-            for b in range(first, first + PAIR):
-                if t == HALVES - 1 and b >= NB // 2:
-                    left_to_vector.append(b)
-                    continue
+
+        def scale_shift_and_project(t, b):
+            half = slice(t * T, (t + 1) * T)
+            if t == HALVES - 1 and b >= NB // 2:
+                nc.vector.tensor_scalar(
+                    y[:, b, half], z[:, b, half], gain_sb[:, b : b + 1], bias_sb[:, b : b + 1], ALU.mult, ALU.add
+                )
+            else:
                 nc.scalar.activation(
                     y[:, b, half], z[:, b, half], ACT.Identity, bias=bias_sb[:, b : b + 1], scale=gain_sb[:, b : b + 1]
                 )
-                project(b, half)
-
-        def project(b, half):
             for h in range(NH):
                 nc.tensor.matmul(
                     logits[h][:, half], wlm_sb[:, b, h:V:NH], y[:, b, half], start=(b == 0), stop=(b == NB - 1)
                 )
 
-        firsts = range(0, NB, PAIR)
-        left_to_vector = []
-        for first in firsts:
-            centre_and_square(0, first)
-        for first in firsts:
-            centre_and_square(1, first)
-            if first == 0:
-                take_rstd(0)
-        for first in firsts:
-            normalise_and_project(0, first)
-            if first == 0:
-                take_rstd(1)
-        for first in firsts:
-            normalise_and_project(1, first)
-        last_half = slice(N - T, N)
-        for b in left_to_vector:
-            nc.vector.tensor_scalar(
-                y[:, b, last_half], z[:, b, last_half], gain_sb[:, b : b + 1], bias_sb[:, b : b + 1], ALU.mult, ALU.add
-            )
-            project(b, last_half)
+        firsts = range(0, NB, GROUP)
+        for q in range(QUARTERS):
+            for first in firsts:
+                centre_and_square(q, first)
+            take_rstd(q)
+        for t in range(HALVES):
+            for q in range(t * QUARTERS // HALVES, (t + 1) * QUARTERS // HALVES):
+                for first in firsts:
+                    normalise(q, first)
+            for b in range(NB):
+                scale_shift_and_project(t, b)
 
         staged = held.tile([P, NH, N], F32, name="staged")
         nc.vector.tensor_copy(staged[:, 0, :], logits[0][:])

@@ -85,7 +85,10 @@ def tile_gatedattentiontransformer_kernel(tc, emb, gain, bias, wlm, offs, out):
                 mean[:, quarter].unsqueeze(1).to_broadcast([P, GROUP, Q]),
                 ALU.subtract,
             )
-            nc.scalar.activation(sq[:, group, quarter], d[:, group, quarter], ACT.Square)
+            if q == QUARTERS - 1 and first == NB - GROUP:
+                nc.vector.tensor_tensor(sq[:, group, quarter], d[:, group, quarter], d[:, group, quarter], ALU.mult)
+            else:
+                nc.scalar.activation(sq[:, group, quarter], d[:, group, quarter], ACT.Square)
             for b in range(first, first + GROUP):
                 nc.tensor.matmul(var[q][:], averager_bf[:], sq[:, b, quarter], start=(b == 0), stop=(b == NB - 1))
 

@@ -107,7 +107,7 @@ def tile_gatedattentiontransformer_kernel(tc, emb, gain, bias, wlm, offs, out):
 
         def scale_shift_and_project(t, b):
             half = slice(t * T, (t + 1) * T)
-            if t == HALVES - 1 and b >= NB // 2:
+            if b >= (2 if t == HALVES - 1 else NB - 2):
                 nc.vector.tensor_scalar(
                     y[:, b, half], z[:, b, half], gain_sb[:, b : b + 1], bias_sb[:, b : b + 1], ALU.mult, ALU.add
                 )

import concourse.mybir as mybir

F32 = mybir.dt.float32
BF16 = mybir.dt.bfloat16
U16 = mybir.dt.uint16
ACT = mybir.ActivationFunctionType
ALU = mybir.AluOpType

P = 128
C = 1024
S = 256
V = 256
N = 128
NB = C // P
NH = V // P
QUARTERS = 4
Q = N // QUARTERS
GROUP = 4
HALVES = 2
T = N // HALVES
EPS = 1e-5

WARMING_MATMULS = 3

FLOPS = 2 * C * V * N


def tile_gatedattentiontransformer_kernel(tc, emb, gain, bias, wlm, offs, out):
    nc = tc.nc
    with (
        tc.tile_pool(name="held", bufs=1) as held,
        tc.tile_pool(name="blocks", bufs=NB) as blocks,
        tc.psum_pool(name="psum", bufs=1) as psum,
    ):
        offsets = held.tile([P, N // 16], U16, name="offsets")
        nc.sync.dma_start(offsets[:], offs)

        emb_blocks = emb.rearrange("(p b) s -> b p s", b=NB)
        tables = []
        for b in range(NB):
            table = blocks.tile([P, S], F32, name="table")
            nc.sync.dma_start(table[:], emb_blocks[b])
            tables.append(table)
        gain_sb = held.tile([P, NB], F32, name="gain_sb")
        nc.sync.dma_start(gain_sb[:], gain.rearrange("(p b) one -> p (b one)", b=NB))
        bias_sb = held.tile([P, NB], F32, name="bias_sb")
        nc.sync.dma_start(bias_sb[:], bias.rearrange("(p b) one -> p (b one)", b=NB))
        wlm_sb = held.tile([P, NB, V], BF16, name="wlm_sb")
        nc.sync.dma_start(wlm_sb[:], wlm.rearrange("(p b) v -> p b v", b=NB))

        averager = held.tile([P, P], F32, name="averager")
        nc.vector.memset(averager[:], 1.0 / C)
        averager_bf = held.tile([P, P], BF16, name="averager_bf")
        nc.vector.memset(averager_bf[:], 1.0 / C)
        eps = held.tile([P, 1], F32, name="eps")
        nc.vector.memset(eps[:], EPS)

        scratch = held.tile([P, 1], F32, name="scratch")
        nc.scalar.activation(scratch[:], eps[:], ACT.Abs_reciprocal_sqrt)

        idle_product = psum.tile([P, P], F32, name="idle_product")
        for i in range(WARMING_MATMULS):
            nc.tensor.matmul(idle_product[:], averager[:], averager[:], start=True, stop=True)

        mean = psum.tile([P, N], F32, name="mean")
        e = held.tile([P, NB, N], F32, name="e")
        for b in range(NB):
            nc.scalar.activation(e[:, b, :], tables[b][:].indirect(offsets[:]), ACT.Copy)
            nc.tensor.matmul(mean[:], averager[:], e[:, b, :], start=(b == 0), stop=(b == NB - 1))

        d = held.tile([P, NB, N], F32, name="d")
        sq = held.tile([P, NB, N], BF16, name="sq")
        z = held.tile([P, NB, N], F32, name="z")
        y = held.tile([P, NB, N], BF16, name="y")
        var = [psum.tile([P, Q], F32, name=f"var{q}") for q in range(QUARTERS)]
        rstd = [held.tile([P, Q], F32, name=f"rstd{q}") for q in range(QUARTERS)]
        logits = [psum.tile([P, N], F32, name=f"logits{h}") for h in range(NH)]

        def centre_and_square(q, first):
            group = slice(first, first + GROUP)
            quarter = slice(q * Q, (q + 1) * Q)
            nc.vector.tensor_tensor(
                d[:, group, quarter],
                e[:, group, quarter],
                mean[:, quarter].unsqueeze(1).to_broadcast([P, GROUP, Q]),
                ALU.subtract,
            )
            if q == QUARTERS - 1 and first == NB - GROUP:
                nc.vector.tensor_tensor(sq[:, group, quarter], d[:, group, quarter], d[:, group, quarter], ALU.mult)
            else:
                nc.scalar.activation(sq[:, group, quarter], d[:, group, quarter], ACT.Square)
            for b in range(first, first + GROUP):
                nc.tensor.matmul(var[q][:], averager_bf[:], sq[:, b, quarter], start=(b == 0), stop=(b == NB - 1))

        def take_rstd(q):
            nc.scalar.activation(rstd[q][:], var[q][:], ACT.Abs_reciprocal_sqrt, bias=eps[:])

        def normalise(q, first):
            group = slice(first, first + GROUP)
            quarter = slice(q * Q, (q + 1) * Q)
            nc.vector.tensor_tensor(
                z[:, group, quarter],
                d[:, group, quarter],
                rstd[q][:].unsqueeze(1).to_broadcast([P, GROUP, Q]),
                ALU.mult,
            )

        def scale_shift_and_project(t, b):
            half = slice(t * T, (t + 1) * T)
            if b >= (2 if t == HALVES - 1 else NB - 2):
                nc.vector.tensor_scalar(
                    y[:, b, half], z[:, b, half], gain_sb[:, b : b + 1], bias_sb[:, b : b + 1], ALU.mult, ALU.add
                )
            else:
                nc.scalar.activation(
                    y[:, b, half], z[:, b, half], ACT.Identity, bias=bias_sb[:, b : b + 1], scale=gain_sb[:, b : b + 1]
                )
            for h in range(NH):
                nc.tensor.matmul(
                    logits[h][:, half], wlm_sb[:, b, h:V:NH], y[:, b, half], start=(b == 0), stop=(b == NB - 1)
                )

        firsts = range(0, NB, GROUP)
        for q in range(QUARTERS):
            for first in firsts:
                centre_and_square(q, first)
            take_rstd(q)
        for t in range(HALVES):
            for q in range(t * QUARTERS // HALVES, (t + 1) * QUARTERS // HALVES):
                for first in firsts:
                    normalise(q, first)
            for b in range(NB):
                scale_shift_and_project(t, b)

        staged = held.tile([P, NH, N], F32, name="staged")
        nc.vector.tensor_copy(staged[:, 0, :], logits[0][:])
        nc.scalar.copy(staged[:, 1, :], logits[1][:])
        nc.sync.dma_start(out.rearrange("(m h) j -> m h j", h=NH), staged[:])
